import numpy as np
import ml_dtypes


def mxq(x, axis, fmt="e4m3"):
    dtype, down = {"e4m3": (ml_dtypes.float8_e4m3fn, 7), "e5m2": (ml_dtypes.float8_e5m2, 14)}[fmt]
    v = np.moveaxis(np.asarray(x, np.float32).astype(ml_dtypes.bfloat16).astype(np.float64), axis, -1)
    blocks = v.reshape(v.shape[:-1] + (-1, 32))
    amax = np.abs(blocks).max(-1, keepdims=True)
    byte = np.maximum(np.where(amax > 0, np.frexp(amax)[1] - 1 + 127, 0) - down, 1)
    scale = np.exp2(byte - 127.0)
    codes = (blocks / scale).astype(np.float32).astype(dtype).astype(np.float64)
    return np.moveaxis((codes * scale).reshape(v.shape), -1, axis)


WIDE = False


def mx_kscale(k):
    if not WIDE:
        return np.ones(k)
    levels = np.array([10, -10, 5, -5, 0])
    if k % 512:
        return np.exp2(np.random.permutation(np.resize(levels, k // 32))).repeat(32)
    a = np.empty((k // 512, 16))
    for p in range(k // 512):
        a[p, :8] = np.random.permutation(np.resize(levels, 8))
        for g in range(8):
            far = levels[np.abs(levels - a[p, g]) >= 10]
            a[p, g + 8] = far[np.random.randint(len(far))]
    return np.exp2(a.ravel()).repeat(32)


BF16 = ml_dtypes.bfloat16


def bf(x):
    return np.asarray(x, np.float32).astype(BF16)


def f64(x):
    return np.asarray(x).astype(np.float64)


B, N, D, L = 2, 4096, 512, 256
SEGS = N // L


def setup_inputs():
    s = mx_kscale(D)
    col = np.concatenate([np.full(D, np.sqrt(SEGS)), np.ones(D)])
    return {"x": bf(np.random.standard_normal((B, N, D)) * s),
            "w_kv": bf(np.random.standard_normal((D, D + D)) * col / np.sqrt(D) / s[:, None])}


def reference(x, w_kv):
    kv = mxq(f64(x), 2, "e4m3") @ mxq(f64(w_kv), 0, "e4m3")
    k, v = kv[..., :D], kv[..., D:]
    keys_lm = k.reshape(B, L, SEGS, D).mean(axis=2)
    vals_lm = v.reshape(B, L, SEGS, D).mean(axis=2)
    return v, keys_lm, vals_lm

@@ -1,0 +1,169 @@
+from contextlib import ExitStack
+
+import concourse.mybir as mybir
+from concourse.masks import make_identity
+
+F32 = mybir.dt.float32
+BF16 = mybir.dt.bfloat16
+U32 = mybir.dt.uint32
+U8 = mybir.dt.uint8
+FP8X4 = mybir.dt.float8_e4m3fn_x4
+
+P = 128
+PACK = 4
+D = 512
+WORDS = D // 2
+TOKENS = 2 * 4096
+SEG = 16
+GROUPS = TOKENS // (P * SEG)
+ROUND = 4
+ROUNDS_PER_GROUP = SEG // ROUND
+ROUNDS = GROUPS * ROUNDS_PER_GROUP
+LOOKAHEAD = 2
+KEYS = 0
+VALUES = 1
+
+FLOPS = 2 * TOKENS * D * 2 * D
+
+
+def tile_ammattention_pa_t_kernel(tc, x, w_kv, out_0, out_1, out_2):
+    nc = tc.nc
+
+    x_groups = x.flatten_outer_dims().rearrange("(g s j) k -> g s (j k)", s=P, j=SEG)
+    v_groups = out_0.flatten_outer_dims().rearrange("(g s j) d -> g s (j d)", s=P, j=SEG)
+    keys_mean_groups = out_1.flatten_outer_dims().rearrange("(g s) d -> g s d", s=P)
+    vals_mean_groups = out_2.flatten_outer_dims().rearrange("(g s) d -> g s d", s=P)
+
+    with ExitStack() as ctx:
+        const = ctx.enter_context(tc.tile_pool(name="const", bufs=1))
+        x_pool = ctx.enter_context(tc.tile_pool(name="x", bufs=GROUPS))
+        grouped_pool = ctx.enter_context(tc.tile_pool(name="grouped", bufs=3))
+        mx_pool = ctx.enter_context(tc.tile_pool(name="mx", bufs=LOOKAHEAD + 2))
+        v_pool = ctx.enter_context(tc.tile_pool(name="v", bufs=5))
+        sum_pool = ctx.enter_context(tc.tile_pool(name="sum", bufs=2))
+        xt_banks = ctx.enter_context(tc.psum_pool(name="xt", bufs=3))
+        v_banks = ctx.enter_context(tc.psum_pool(name="vb", bufs=3))
+        keys_banks = ctx.enter_context(tc.psum_pool(name="kb", bufs=2))
+        ctx.enter_context(tc.manual_schedule())
+
+        x_tiles = [x_pool.tile([P, SEG * D], BF16, name="x_tile") for g in range(GROUPS)]
+
+        def load_x(g, first_round, rounds):
+            cols = slice(first_round * ROUND * D, (first_round + rounds) * ROUND * D)
+            nc.sync.dma_start(out=x_tiles[g][:, cols], in_=x_groups[g, :, cols])
+
+        load_x(0, 0, 1)
+        w_rows = const.tile([P, PACK, 2 * D], BF16)
+        nc.sync.dma_start(out=w_rows[:], in_=w_kv.rearrange("(p t) c -> p t c", t=PACK))
+        for r in range(1, ROUNDS_PER_GROUP):
+            load_x(0, r, 1)
+        for g in range(1, GROUPS):
+            load_x(g, 0, ROUNDS_PER_GROUP)
+
+        ident = const.tile([P, P], F32)
+        make_identity(nc, ident[:])
+
+        def transpose_round(r):
+            g, in_group = divmod(r, ROUNDS_PER_GROUP)
+            words = x_tiles[g][:].bitcast(F32)
+            grouped = grouped_pool.tile([P, ROUND * P * PACK], BF16, align_bytes=64)
+            grouped_words = grouped[:].bitcast(F32).rearrange("p (j s u) -> p j s u", j=ROUND, u=2)
+            for pair in range(ROUND // 2):
+                xt = xt_banks.tile([P, 2, 2, P], F32)
+                for jj in range(2):
+                    for u in range(2):
+                        first = (in_group * ROUND + 2 * pair + jj) * WORDS
+                        every_second = slice(first + u, first + WORDS, 2)
+                        nc.tensor.transpose(xt[:, jj, u, :], words[:, every_second], ident[:])
+                nc.scalar.copy(
+                    out=grouped_words[:, 2 * pair : 2 * pair + 2],
+                    in_=xt[:].rearrange("p j u s -> p j s u"),
+                )
+            return grouped
+
+        quantised = []
+
+        def quantise_round(grouped):
+            codes = mx_pool.tile([P, ROUND * P], U32, align_bytes=64)
+            scales = mx_pool.tile([P, ROUND * P], U8, align_bytes=64)
+            nc.vector.quantize_mx(out=codes[:].bitcast(FP8X4), scales=scales[:], in_=grouped[:])
+            quantised.append((codes, scales))
+
+        grouped = transpose_round(0)
+
+        w_grouped = const.tile([P, 2, D, PACK], BF16, align_bytes=64)
+        w_codes = const.tile([P, 2, D], U32, align_bytes=64)
+        w_scales = const.tile([P, 2, D], U8, align_bytes=64)
+        nc.vector.tensor_copy(
+            out=w_grouped[:, KEYS].rearrange("p (c i) t -> p c t i", i=4),
+            in_=w_rows[:, :, 0:D].rearrange("p t (c i) -> p c t i", i=4),
+        )
+        nc.scalar.copy(
+            out=w_grouped[:, VALUES].rearrange("p (c i) t -> p c t i", i=4),
+            in_=w_rows[:, :, D : 2 * D].rearrange("p t (c i) -> p c t i", i=4),
+        )
+        quantise_round(grouped)
+        for half in (KEYS, VALUES):
+            nc.vector.quantize_mx(
+                out=w_codes[:, half].bitcast(FP8X4),
+                scales=w_scales[:, half],
+                in_=w_grouped[:, half].rearrange("p c t -> p (c t)"),
+            )
+        for r in range(1, LOOKAHEAD):
+            quantise_round(transpose_round(r))
+
+        keys_sum = None
+        first_pair = None
+        vals_sum = None
+        for r in range(ROUNDS):
+            g, in_group = divmod(r, ROUNDS_PER_GROUP)
+            if r + LOOKAHEAD < ROUNDS:
+                quantise_round(transpose_round(r + LOOKAHEAD))
+            codes, scales = quantised[r]
+
+            if in_group == 0:
+                keys_sum = keys_banks.tile([P, D], F32)
+                vals_sum = sum_pool.tile([P, 2 * D], F32)
+            v_rows = v_pool.tile([P, ROUND * D], F32)
+            for jj in range(ROUND):
+                j = in_group * ROUND + jj
+                segs = slice(jj * P, (jj + 1) * P)
+                nc.tensor.matmul_mx(
+                    out=keys_sum[:],
+                    lhsT=codes[:, segs].bitcast(FP8X4),
+                    lhsT_scale=scales[:, segs],
+                    rhs=w_codes[:, KEYS].bitcast(FP8X4),
+                    rhs_scale=w_scales[:, KEYS],
+                    start=(j == 0),
+                    stop=(j == SEG - 1),
+                )
+                if j == SEG - 1:
+                    keys_mean = sum_pool.tile([P, D], F32)
+                    nc.vector.tensor_scalar_mul(out=keys_mean[:], in0=keys_sum[:], scalar1=1.0 / SEG)
+                    nc.sync.dma_start(out=keys_mean_groups[g], in_=keys_mean[:])
+                v_bank = v_banks.tile([P, D], F32)
+                nc.tensor.matmul_mx(
+                    out=v_bank[:],
+                    lhsT=codes[:, segs].bitcast(FP8X4),
+                    lhsT_scale=scales[:, segs],
+                    rhs=w_codes[:, VALUES].bitcast(FP8X4),
+                    rhs_scale=w_scales[:, VALUES],
+                    start=True,
+                    stop=True,
+                )
+                nc.scalar.copy(out=v_rows[:, jj * D : (jj + 1) * D], in_=v_bank[:])
+                if jj % 2 == 1:
+                    pair = v_rows[:, (jj - 1) * D : (jj + 1) * D]
+                    nc.sync.dma_start(out=v_groups[g, :, (j - 1) * D : (j + 1) * D], in_=pair)
+                    if j == 1:
+                        first_pair = pair
+                    elif j == 3:
+                        nc.vector.tensor_add(out=vals_sum[:], in0=first_pair, in1=pair)
+                    else:
+                        nc.vector.tensor_add(out=vals_sum[:], in0=vals_sum[:], in1=pair)
+
+            if in_group == ROUNDS_PER_GROUP - 1:
+                vals_mean = sum_pool.tile([P, D], F32)
+                nc.vector.tensor_add(out=vals_mean[:], in0=vals_sum[:, 0:D], in1=vals_sum[:, D : 2 * D])
+                nc.vector.tensor_scalar_mul(out=vals_mean[:], in0=vals_mean[:], scalar1=1.0 / SEG)
+                nc.sync.dma_start(out=vals_mean_groups[g], in_=vals_mean[:])

@@ -22,6 +22,9 @@ ROUNDS = GROUPS * ROUNDS_PER_GROUP
 LOOKAHEAD = 2
 KEYS = 0
 VALUES = 1
+ADD = mybir.AluOpType.add
+MULT = mybir.AluOpType.mult
+COPY = mybir.ActivationFunctionType.Copy
 
 FLOPS = 2 * TOKENS * D * 2 * D
 
@@ -112,58 +115,79 @@ def tile_ammattention_pa_t_kernel(tc, x, w_kv, out_0, out_1, out_2):
         for r in range(1, LOOKAHEAD):
             quantise_round(transpose_round(r))
 
-        keys_sum = None
+        def multiply(out, r, jj, half, start, stop):
+            codes, scales = quantised[r]
+            segs = slice(jj * P, (jj + 1) * P)
+            nc.tensor.matmul_mx(
+                out=out,
+                lhsT=codes[:, segs].bitcast(FP8X4),
+                lhsT_scale=scales[:, segs],
+                rhs=w_codes[:, half].bitcast(FP8X4),
+                rhs_scale=w_scales[:, half],
+                start=start,
+                stop=stop,
+            )
+
+        keys_sums = {}
+
+        def keys_pass(r, jj):
+            g, j = divmod(r * ROUND + jj, SEG)
+            if j == 0:
+                keys_sums[g] = keys_banks.tile([P, D], F32, name="keys_sum")
+            multiply(keys_sums[g][:], r, jj, KEYS, j == 0, j == SEG - 1)
+            if j == SEG - 1:
+                keys_mean = sum_pool.tile([P, D], F32)
+                if g < GROUPS - 1:
+                    nc.vector.tensor_scalar_mul(out=keys_mean[:], in0=keys_sums[g][:], scalar1=1.0 / SEG)
+                else:
+                    nc.scalar.activation(out=keys_mean[:], in_=keys_sums[g][:], func=COPY, scale=1.0 / SEG)
+                nc.sync.dma_start(out=keys_mean_groups[g], in_=keys_mean[:])
+
         first_pair = None
         vals_sum = None
+        tail_sum = None
+        vals_means = {}
         for r in range(ROUNDS):
             g, in_group = divmod(r, ROUNDS_PER_GROUP)
             if r + LOOKAHEAD < ROUNDS:
                 quantise_round(transpose_round(r + LOOKAHEAD))
-            codes, scales = quantised[r]
 
             if in_group == 0:
-                keys_sum = keys_banks.tile([P, D], F32)
                 vals_sum = sum_pool.tile([P, 2 * D], F32)
+            if r == ROUNDS - 1:
+                for jj in range(ROUND):
+                    keys_pass(r, jj)
+                tail_sum = xt_banks.tile([P, D], F32, name="xt")
             v_rows = v_pool.tile([P, ROUND * D], F32)
             for jj in range(ROUND):
                 j = in_group * ROUND + jj
-                segs = slice(jj * P, (jj + 1) * P)
-                nc.tensor.matmul_mx(
-                    out=keys_sum[:],
-                    lhsT=codes[:, segs].bitcast(FP8X4),
-                    lhsT_scale=scales[:, segs],
-                    rhs=w_codes[:, KEYS].bitcast(FP8X4),
-                    rhs_scale=w_scales[:, KEYS],
-                    start=(j == 0),
-                    stop=(j == SEG - 1),
-                )
-                if j == SEG - 1:
-                    keys_mean = sum_pool.tile([P, D], F32)
-                    nc.vector.tensor_scalar_mul(out=keys_mean[:], in0=keys_sum[:], scalar1=1.0 / SEG)
-                    nc.sync.dma_start(out=keys_mean_groups[g], in_=keys_mean[:])
+                if r < ROUNDS - 1:
+                    keys_pass(r, jj)
+                else:
+                    multiply(tail_sum[:], r, jj, VALUES, jj == 0, jj == ROUND - 1)
                 v_bank = v_banks.tile([P, D], F32)
-                nc.tensor.matmul_mx(
-                    out=v_bank[:],
-                    lhsT=codes[:, segs].bitcast(FP8X4),
-                    lhsT_scale=scales[:, segs],
-                    rhs=w_codes[:, VALUES].bitcast(FP8X4),
-                    rhs_scale=w_scales[:, VALUES],
-                    start=True,
-                    stop=True,
-                )
+                multiply(v_bank[:], r, jj, VALUES, True, True)
                 nc.scalar.copy(out=v_rows[:, jj * D : (jj + 1) * D], in_=v_bank[:])
-                if jj % 2 == 1:
+                if r == ROUNDS - 1 and jj >= ROUND - 2:
+                    nc.sync.dma_start(out=v_groups[g, :, j * D : (j + 1) * D], in_=v_rows[:, jj * D : (jj + 1) * D])
+                elif jj % 2 == 1:
                     pair = v_rows[:, (jj - 1) * D : (jj + 1) * D]
                     nc.sync.dma_start(out=v_groups[g, :, (j - 1) * D : (j + 1) * D], in_=pair)
+                    if j == 5 and g > 0:
+                        nc.sync.dma_start(out=vals_mean_groups[g - 1], in_=vals_means[g - 1][:])
                     if j == 1:
                         first_pair = pair
                     elif j == 3:
                         nc.vector.tensor_add(out=vals_sum[:], in0=first_pair, in1=pair)
-                    else:
+                    elif r < ROUNDS - 1:
                         nc.vector.tensor_add(out=vals_sum[:], in0=vals_sum[:], in1=pair)
-
-            if in_group == ROUNDS_PER_GROUP - 1:
-                vals_mean = sum_pool.tile([P, D], F32)
-                nc.vector.tensor_add(out=vals_mean[:], in0=vals_sum[:, 0:D], in1=vals_sum[:, D : 2 * D])
-                nc.vector.tensor_scalar_mul(out=vals_mean[:], in0=vals_mean[:], scalar1=1.0 / SEG)
-                nc.sync.dma_start(out=vals_mean_groups[g], in_=vals_mean[:])
+                if j == SEG - 1 and r < ROUNDS - 1 or r == ROUNDS - 2 and jj == ROUND - 1:
+                    mean = sum_pool.tile([P, D], F32, name="vals_mean")
+                    vals_means[g] = mean
+                    nc.vector.tensor_add(out=mean[:], in0=vals_sum[:, 0:D], in1=vals_sum[:, D : 2 * D])
+                    nc.vector.tensor_scalar_mul(out=mean[:], in0=mean[:], scalar1=1.0 / SEG)
+        mean = vals_means[GROUPS - 1]
+        nc.vector.scalar_tensor_tensor(
+            out=mean[:], in0=tail_sum[:], scalar=1.0 / SEG, op0=MULT, in1=mean[:], op1=ADD
+        )
+        nc.sync.dma_start(out=vals_mean_groups[GROUPS - 1], in_=mean[:])

@@ -66,6 +66,14 @@ def tile_ammattention_pa_t_kernel(tc, x, w_kv, out_0, out_1, out_2):
         ident = const.tile([P, P], F32)
         make_identity(nc, ident[:])
 
+        zeros = const.tile([P, D], BF16)
+        nc.vector.memset(zeros[:], 0.0)
+
+        def warm_up(passes):
+            nowhere = v_banks.tile([P, D], F32, name="v_bank")
+            for i in range(passes):
+                nc.tensor.matmul(out=nowhere[:], lhsT=zeros[:, 0:P], rhs=zeros[:], start=True, stop=True)
+
         def transpose_round(r):
             g, in_group = divmod(r, ROUNDS_PER_GROUP)
             words = x_tiles[g][:].bitcast(F32)
@@ -92,7 +100,9 @@ def tile_ammattention_pa_t_kernel(tc, x, w_kv, out_0, out_1, out_2):
             nc.vector.quantize_mx(out=codes[:].bitcast(FP8X4), scales=scales[:], in_=grouped[:])
             quantised.append((codes, scales))
 
+        warm_up(7)
         grouped = transpose_round(0)
+        warm_up(5)
 
         w_grouped = const.tile([P, 2, D, PACK], BF16, align_bytes=64)
         w_codes = const.tile([P, 2, D], U32, align_bytes=64)
@@ -114,6 +124,7 @@ def tile_ammattention_pa_t_kernel(tc, x, w_kv, out_0, out_1, out_2):
             )
         for r in range(1, LOOKAHEAD):
             quantise_round(transpose_round(r))
+            warm_up(2)
 
         def multiply(out, r, jj, half, start, stop):
             codes, scales = quantised[r]
@@ -151,6 +162,8 @@ def tile_ammattention_pa_t_kernel(tc, x, w_kv, out_0, out_1, out_2):
             g, in_group = divmod(r, ROUNDS_PER_GROUP)
             if r + LOOKAHEAD < ROUNDS:
                 quantise_round(transpose_round(r + LOOKAHEAD))
+            if r == 0:
+                warm_up(2)
 
             if in_group == 0:
                 vals_sum = sum_pool.tile([P, 2 * D], F32)

@@ -24,6 +24,7 @@ KEYS = 0
 VALUES = 1
 ADD = mybir.AluOpType.add
 MULT = mybir.AluOpType.mult
+SUM_NAMES = ("first_sum", "second_sum")
 COPY = mybir.ActivationFunctionType.Copy
 
 FLOPS = 2 * TOKENS * D * 2 * D
@@ -40,6 +41,7 @@ def tile_ammattention_pa_t_kernel(tc, x, w_kv, out_0, out_1, out_2):
     with ExitStack() as ctx:
         const = ctx.enter_context(tc.tile_pool(name="const", bufs=1))
         x_pool = ctx.enter_context(tc.tile_pool(name="x", bufs=GROUPS))
+        w_pool = ctx.enter_context(tc.tile_pool(name="w", bufs=2))
         grouped_pool = ctx.enter_context(tc.tile_pool(name="grouped", bufs=3))
         mx_pool = ctx.enter_context(tc.tile_pool(name="mx", bufs=LOOKAHEAD + 2))
         v_pool = ctx.enter_context(tc.tile_pool(name="v", bufs=5))
@@ -55,10 +57,19 @@ def tile_ammattention_pa_t_kernel(tc, x, w_kv, out_0, out_1, out_2):
             cols = slice(first_round * ROUND * D, (first_round + rounds) * ROUND * D)
             nc.sync.dma_start(out=x_tiles[g][:, cols], in_=x_groups[g, :, cols])
 
+        w_rows = [w_pool.tile([P, PACK, D], BF16, name="w_rows") for half in (KEYS, VALUES)]
+
+        def load_w(half):
+            cols = slice(half * D, (half + 1) * D)
+            nc.sync.dma_start(
+                out=w_rows[half][:], in_=w_kv.rearrange("(p t) c -> p t c", t=PACK)[:, :, cols]
+            )
+
         load_x(0, 0, 1)
-        w_rows = const.tile([P, PACK, 2 * D], BF16)
-        nc.sync.dma_start(out=w_rows[:], in_=w_kv.rearrange("(p t) c -> p t c", t=PACK))
-        for r in range(1, ROUNDS_PER_GROUP):
+        load_w(VALUES)
+        load_x(0, 1, 1)
+        load_w(KEYS)
+        for r in range(2, ROUNDS_PER_GROUP):
             load_x(0, r, 1)
         for g in range(1, GROUPS):
             load_x(g, 0, ROUNDS_PER_GROUP)
@@ -100,31 +111,34 @@ def tile_ammattention_pa_t_kernel(tc, x, w_kv, out_0, out_1, out_2):
             nc.vector.quantize_mx(out=codes[:].bitcast(FP8X4), scales=scales[:], in_=grouped[:])
             quantised.append((codes, scales))
 
-        warm_up(7)
-        grouped = transpose_round(0)
-        warm_up(5)
-
         w_grouped = const.tile([P, 2, D, PACK], BF16, align_bytes=64)
         w_codes = const.tile([P, 2, D], U32, align_bytes=64)
         w_scales = const.tile([P, 2, D], U8, align_bytes=64)
-        nc.vector.tensor_copy(
-            out=w_grouped[:, KEYS].rearrange("p (c i) t -> p c t i", i=4),
-            in_=w_rows[:, :, 0:D].rearrange("p t (c i) -> p c t i", i=4),
-        )
-        nc.scalar.copy(
-            out=w_grouped[:, VALUES].rearrange("p (c i) t -> p c t i", i=4),
-            in_=w_rows[:, :, D : 2 * D].rearrange("p t (c i) -> p c t i", i=4),
-        )
-        quantise_round(grouped)
-        for half in (KEYS, VALUES):
+
+        def regroup_w(half):
+            nc.vector.tensor_copy(
+                out=w_grouped[:, half].rearrange("p (c i) t -> p c t i", i=4),
+                in_=w_rows[half][:].rearrange("p t (c i) -> p c t i", i=4),
+            )
+
+        def quantise_w(half):
             nc.vector.quantize_mx(
                 out=w_codes[:, half].bitcast(FP8X4),
                 scales=w_scales[:, half],
                 in_=w_grouped[:, half].rearrange("p c t -> p (c t)"),
             )
-        for r in range(1, LOOKAHEAD):
-            quantise_round(transpose_round(r))
-            warm_up(2)
+
+        warm_up(5)
+        grouped = transpose_round(0)
+        regroup_w(VALUES)
+        quantise_round(grouped)
+        quantise_w(VALUES)
+        warm_up(3)
+        grouped = transpose_round(1)
+        warm_up(2)
+        regroup_w(KEYS)
+        quantise_w(KEYS)
+        quantise_round(grouped)
 
         def multiply(out, r, jj, half, start, stop):
             codes, scales = quantised[r]
@@ -154,19 +168,21 @@ def tile_ammattention_pa_t_kernel(tc, x, w_kv, out_0, out_1, out_2):
                     nc.scalar.activation(out=keys_mean[:], in_=keys_sums[g][:], func=COPY, scale=1.0 / SEG)
                 nc.sync.dma_start(out=keys_mean_groups[g], in_=keys_mean[:])
 
-        first_pair = None
-        vals_sum = None
+        vals_sums = [None, None]
         tail_sum = None
         vals_means = {}
+        LAST = ROUNDS - 2
+
+        def join_mean(mean, values):
+            nc.vector.scalar_tensor_tensor(
+                out=mean[:], in0=values, scalar=1.0 / SEG, op0=MULT, in1=mean[:], op1=ADD
+            )
+
         for r in range(ROUNDS):
             g, in_group = divmod(r, ROUNDS_PER_GROUP)
-            if r + LOOKAHEAD < ROUNDS:
+            if 0 < r < ROUNDS - LOOKAHEAD:
                 quantise_round(transpose_round(r + LOOKAHEAD))
-            if r == 0:
-                warm_up(2)
 
-            if in_group == 0:
-                vals_sum = sum_pool.tile([P, 2 * D], F32)
             if r == ROUNDS - 1:
                 for jj in range(ROUND):
                     keys_pass(r, jj)
@@ -174,9 +190,9 @@ def tile_ammattention_pa_t_kernel(tc, x, w_kv, out_0, out_1, out_2):
             v_rows = v_pool.tile([P, ROUND * D], F32)
             for jj in range(ROUND):
                 j = in_group * ROUND + jj
-                if r < ROUNDS - 1:
+                if 0 < r < ROUNDS - 1:
                     keys_pass(r, jj)
-                else:
+                elif r > 0:
                     multiply(tail_sum[:], r, jj, VALUES, jj == 0, jj == ROUND - 1)
                 v_bank = v_banks.tile([P, D], F32)
                 multiply(v_bank[:], r, jj, VALUES, True, True)
@@ -185,22 +201,43 @@ def tile_ammattention_pa_t_kernel(tc, x, w_kv, out_0, out_1, out_2):
                     nc.sync.dma_start(out=v_groups[g, :, j * D : (j + 1) * D], in_=v_rows[:, jj * D : (jj + 1) * D])
                 elif jj % 2 == 1:
                     pair = v_rows[:, (jj - 1) * D : (jj + 1) * D]
-                    nc.sync.dma_start(out=v_groups[g, :, (j - 1) * D : (j + 1) * D], in_=pair)
-                    if j == 5 and g > 0:
-                        nc.sync.dma_start(out=vals_mean_groups[g - 1], in_=vals_means[g - 1][:])
-                    if j == 1:
-                        first_pair = pair
-                    elif j == 3:
-                        nc.vector.tensor_add(out=vals_sum[:], in0=first_pair, in1=pair)
-                    elif r < ROUNDS - 1:
-                        nc.vector.tensor_add(out=vals_sum[:], in0=vals_sum[:], in1=pair)
-                if j == SEG - 1 and r < ROUNDS - 1 or r == ROUNDS - 2 and jj == ROUND - 1:
-                    mean = sum_pool.tile([P, D], F32, name="vals_mean")
-                    vals_means[g] = mean
-                    nc.vector.tensor_add(out=mean[:], in0=vals_sum[:, 0:D], in1=vals_sum[:, D : 2 * D])
+                    if r >= ROUNDS - 2:
+                        nc.sync.dma_start(out=v_groups[g, :, (j - 1) * D : (j + 1) * D], in_=pair)
+                    elif jj == ROUND - 1:
+                        nc.sync.dma_start(out=v_groups[g, :, (j + 1 - ROUND) * D : (j + 1) * D], in_=v_rows[:])
+                    if j == 7 and g > 0:
+                        nc.sync.dma_start(out=vals_mean_groups[g - 1], in_=vals_means[g - 1][0][:])
+                    which = jj // 2
+                    if in_group == 0:
+                        vals_sums[which] = pair
+                    elif r < LAST:
+                        before = vals_sums[which]
+                        if in_group == 1:
+                            running = sum_pool.tile([P, 2 * D], F32, name=SUM_NAMES[which])
+                            vals_sums[which] = running[:]
+                        nc.vector.tensor_add(out=vals_sums[which], in0=before, in1=pair)
+                if r == LAST:
+                    join_mean(vals_means[g][jj % 2], v_rows[:, jj * D : (jj + 1) * D])
+            if r == 0:
+                quantise_round(transpose_round(LOOKAHEAD))
+                for jj in range(ROUND):
+                    keys_pass(r, jj)
+            if in_group == ROUNDS_PER_GROUP - 1 and r < LAST:
+                total = vals_sums[0]
+                nc.vector.tensor_add(out=total, in0=total, in1=vals_sums[1])
+                vals_means[g] = [sum_pool.tile([P, D], F32, name="mean", bufs=3)]
+                mean = vals_means[g][0]
+                nc.vector.tensor_add(out=mean[:], in0=total[:, 0:D], in1=total[:, D : 2 * D])
+                nc.vector.tensor_scalar_mul(out=mean[:], in0=mean[:], scalar1=1.0 / SEG)
+            elif r == LAST - 1:
+                vals_means[g] = [sum_pool.tile([P, D], F32, name="mean", bufs=3) for total in vals_sums]
+                for mean, total in zip(vals_means[g], vals_sums):
+                    nc.vector.tensor_add(out=mean[:], in0=total[:, 0:D], in1=total[:, D : 2 * D])
+                for mean in vals_means[g]:
                     nc.vector.tensor_scalar_mul(out=mean[:], in0=mean[:], scalar1=1.0 / SEG)
-        mean = vals_means[GROUPS - 1]
-        nc.vector.scalar_tensor_tensor(
-            out=mean[:], in0=tail_sum[:], scalar=1.0 / SEG, op0=MULT, in1=mean[:], op1=ADD
-        )
+            elif r == LAST:
+                mean, other = vals_means[g]
+                nc.vector.tensor_add(out=mean[:], in0=mean[:], in1=other[:])
+        mean = vals_means[GROUPS - 1][0]
+        join_mean(mean, tail_sum[:])
         nc.sync.dma_start(out=vals_mean_groups[GROUPS - 1], in_=mean[:])

@@ -24,7 +24,7 @@ KEYS = 0
 VALUES = 1
 ADD = mybir.AluOpType.add
 MULT = mybir.AluOpType.mult
-SUM_NAMES = ("first_sum", "second_sum")
+SUM_NAMES = ("even_sum", "odd_sum")
 COPY = mybir.ActivationFunctionType.Copy
 
 FLOPS = 2 * TOKENS * D * 2 * D
@@ -44,7 +44,7 @@ def tile_ammattention_pa_t_kernel(tc, x, w_kv, out_0, out_1, out_2):
         w_pool = ctx.enter_context(tc.tile_pool(name="w", bufs=2))
         grouped_pool = ctx.enter_context(tc.tile_pool(name="grouped", bufs=3))
         mx_pool = ctx.enter_context(tc.tile_pool(name="mx", bufs=LOOKAHEAD + 2))
-        v_pool = ctx.enter_context(tc.tile_pool(name="v", bufs=5))
+        v_pool = ctx.enter_context(tc.tile_pool(name="v", bufs=9))
         sum_pool = ctx.enter_context(tc.tile_pool(name="sum", bufs=2))
         xt_banks = ctx.enter_context(tc.psum_pool(name="xt", bufs=3))
         v_banks = ctx.enter_context(tc.psum_pool(name="vb", bufs=3))
@@ -164,25 +164,22 @@ def tile_ammattention_pa_t_kernel(tc, x, w_kv, out_0, out_1, out_2):
                 keys_mean = sum_pool.tile([P, D], F32)
                 if g < GROUPS - 1:
                     nc.vector.tensor_scalar_mul(out=keys_mean[:], in0=keys_sums[g][:], scalar1=1.0 / SEG)
+                    nc.gpsimd.dma_start(out=keys_mean_groups[g], in_=keys_mean[:])
                 else:
                     nc.scalar.activation(out=keys_mean[:], in_=keys_sums[g][:], func=COPY, scale=1.0 / SEG)
-                nc.sync.dma_start(out=keys_mean_groups[g], in_=keys_mean[:])
+                    nc.sync.dma_start(out=keys_mean_groups[g], in_=keys_mean[:])
 
-        vals_sums = [None, None]
+        first_pair = None
+        vals_sum = None
+        last_sums = [None, None]
         tail_sum = None
-        vals_means = {}
-        LAST = ROUNDS - 2
-
-        def join_mean(mean, values):
-            nc.vector.scalar_tensor_tensor(
-                out=mean[:], in0=values, scalar=1.0 / SEG, op0=MULT, in1=mean[:], op1=ADD
-            )
-
         for r in range(ROUNDS):
             g, in_group = divmod(r, ROUNDS_PER_GROUP)
             if 0 < r < ROUNDS - LOOKAHEAD:
                 quantise_round(transpose_round(r + LOOKAHEAD))
 
+            if in_group == 0 and g < GROUPS - 1:
+                vals_sum = sum_pool.tile([P, 2 * D], F32)
             if r == ROUNDS - 1:
                 for jj in range(ROUND):
                     keys_pass(r, jj)
@@ -201,43 +198,38 @@ def tile_ammattention_pa_t_kernel(tc, x, w_kv, out_0, out_1, out_2):
                     nc.sync.dma_start(out=v_groups[g, :, j * D : (j + 1) * D], in_=v_rows[:, jj * D : (jj + 1) * D])
                 elif jj % 2 == 1:
                     pair = v_rows[:, (jj - 1) * D : (jj + 1) * D]
-                    if r >= ROUNDS - 2:
+                    if g == GROUPS - 1:
                         nc.sync.dma_start(out=v_groups[g, :, (j - 1) * D : (j + 1) * D], in_=pair)
                     elif jj == ROUND - 1:
                         nc.sync.dma_start(out=v_groups[g, :, (j + 1 - ROUND) * D : (j + 1) * D], in_=v_rows[:])
-                    if j == 7 and g > 0:
-                        nc.sync.dma_start(out=vals_mean_groups[g - 1], in_=vals_means[g - 1][0][:])
-                    which = jj // 2
-                    if in_group == 0:
-                        vals_sums[which] = pair
-                    elif r < LAST:
-                        before = vals_sums[which]
-                        if in_group == 1:
-                            running = sum_pool.tile([P, 2 * D], F32, name=SUM_NAMES[which])
-                            vals_sums[which] = running[:]
-                        nc.vector.tensor_add(out=vals_sums[which], in0=before, in1=pair)
-                if r == LAST:
-                    join_mean(vals_means[g][jj % 2], v_rows[:, jj * D : (jj + 1) * D])
+                    if j == 1:
+                        first_pair = pair
+                    elif g < GROUPS - 1:
+                        before = first_pair if j == 3 else vals_sum[:]
+                        nc.vector.tensor_add(out=vals_sum[:], in0=before, in1=pair)
+                if g == GROUPS - 1 and r < ROUNDS - 1:
+                    before = last_sums[jj % 2]
+                    v_slice = v_rows[:, jj * D : (jj + 1) * D]
+                    if j < 2:
+                        last_sums[jj % 2] = v_slice
+                    else:
+                        if j < 4:
+                            running = sum_pool.tile([P, D], F32, name=SUM_NAMES[jj % 2])
+                            last_sums[jj % 2] = running[:]
+                        nc.vector.tensor_add(out=last_sums[jj % 2], in0=before, in1=v_slice)
             if r == 0:
                 quantise_round(transpose_round(LOOKAHEAD))
                 for jj in range(ROUND):
                     keys_pass(r, jj)
-            if in_group == ROUNDS_PER_GROUP - 1 and r < LAST:
-                total = vals_sums[0]
-                nc.vector.tensor_add(out=total, in0=total, in1=vals_sums[1])
-                vals_means[g] = [sum_pool.tile([P, D], F32, name="mean", bufs=3)]
-                mean = vals_means[g][0]
-                nc.vector.tensor_add(out=mean[:], in0=total[:, 0:D], in1=total[:, D : 2 * D])
+            if in_group == ROUNDS_PER_GROUP - 1 and g < GROUPS - 1:
+                mean = sum_pool.tile([P, D], F32, name="vals_mean")
+                nc.vector.tensor_add(out=mean[:], in0=vals_sum[:, 0:D], in1=vals_sum[:, D : 2 * D])
                 nc.vector.tensor_scalar_mul(out=mean[:], in0=mean[:], scalar1=1.0 / SEG)
-            elif r == LAST - 1:
-                vals_means[g] = [sum_pool.tile([P, D], F32, name="mean", bufs=3) for total in vals_sums]
-                for mean, total in zip(vals_means[g], vals_sums):
-                    nc.vector.tensor_add(out=mean[:], in0=total[:, 0:D], in1=total[:, D : 2 * D])
-                for mean in vals_means[g]:
-                    nc.vector.tensor_scalar_mul(out=mean[:], in0=mean[:], scalar1=1.0 / SEG)
-            elif r == LAST:
-                mean, other = vals_means[g]
-                nc.vector.tensor_add(out=mean[:], in0=mean[:], in1=other[:])
-        mean = vals_means[GROUPS - 1][0]
-        join_mean(mean, tail_sum[:])
+                nc.gpsimd.dma_start(out=vals_mean_groups[g], in_=mean[:])
+        mean = sum_pool.tile([P, D], F32, name="vals_mean")
+        nc.vector.tensor_add(out=mean[:], in0=last_sums[0], in1=last_sums[1])
+        nc.vector.tensor_scalar_mul(out=mean[:], in0=mean[:], scalar1=1.0 / SEG)
+        nc.vector.scalar_tensor_tensor(
+            out=mean[:], in0=tail_sum[:], scalar=1.0 / SEG, op0=MULT, in1=mean[:], op1=ADD
+        )
         nc.sync.dma_start(out=vals_mean_groups[GROUPS - 1], in_=mean[:])

@@ -46,8 +46,8 @@ def tile_ammattention_pa_t_kernel(tc, x, w_kv, out_0, out_1, out_2):
         mx_pool = ctx.enter_context(tc.tile_pool(name="mx", bufs=LOOKAHEAD + 2))
         v_pool = ctx.enter_context(tc.tile_pool(name="v", bufs=9))
         sum_pool = ctx.enter_context(tc.tile_pool(name="sum", bufs=2))
-        xt_banks = ctx.enter_context(tc.psum_pool(name="xt", bufs=3))
-        v_banks = ctx.enter_context(tc.psum_pool(name="vb", bufs=3))
+        xt_banks = ctx.enter_context(tc.psum_pool(name="xt", bufs=2))
+        v_banks = ctx.enter_context(tc.psum_pool(name="vb", bufs=4))
         keys_banks = ctx.enter_context(tc.psum_pool(name="kb", bufs=2))
         ctx.enter_context(tc.manual_schedule())
 
@@ -106,14 +106,14 @@ def tile_ammattention_pa_t_kernel(tc, x, w_kv, out_0, out_1, out_2):
         quantised = []
 
         def quantise_round(grouped):
-            codes = mx_pool.tile([P, ROUND * P], U32, align_bytes=64)
-            scales = mx_pool.tile([P, ROUND * P], U8, align_bytes=64)
+            codes = mx_pool.tile([P, ROUND * P], U32, align_bytes=256)
+            scales = mx_pool.tile([P, ROUND * P], U8, align_bytes=256)
             nc.vector.quantize_mx(out=codes[:].bitcast(FP8X4), scales=scales[:], in_=grouped[:])
             quantised.append((codes, scales))
 
         w_grouped = const.tile([P, 2, D, PACK], BF16, align_bytes=64)
-        w_codes = const.tile([P, 2, D], U32, align_bytes=64)
-        w_scales = const.tile([P, 2, D], U8, align_bytes=64)
+        w_codes = const.tile([P, 2, D], U32, align_bytes=256)
+        w_scales = const.tile([P, 2, D], U8, align_bytes=256)
 
         def regroup_w(half):
             nc.vector.tensor_copy(

@@ -22,6 +22,8 @@ ROUNDS = GROUPS * ROUNDS_PER_GROUP
 LOOKAHEAD = 2
 KEYS = 0
 VALUES = 1
+SORT_AHEAD = 5
+FINE = ROUNDS // 2
 ADD = mybir.AluOpType.add
 MULT = mybir.AluOpType.mult
 SUM_NAMES = ("even_sum", "odd_sum")
@@ -43,6 +45,7 @@ def tile_ammattention_pa_t_kernel(tc, x, w_kv, out_0, out_1, out_2):
         x_pool = ctx.enter_context(tc.tile_pool(name="x", bufs=GROUPS))
         w_pool = ctx.enter_context(tc.tile_pool(name="w", bufs=2))
         grouped_pool = ctx.enter_context(tc.tile_pool(name="grouped", bufs=3))
+        sorted_pool = ctx.enter_context(tc.tile_pool(name="sorted", bufs=2))
         mx_pool = ctx.enter_context(tc.tile_pool(name="mx", bufs=LOOKAHEAD + 2))
         v_pool = ctx.enter_context(tc.tile_pool(name="v", bufs=9))
         sum_pool = ctx.enter_context(tc.tile_pool(name="sum", bufs=2))
@@ -85,6 +88,15 @@ def tile_ammattention_pa_t_kernel(tc, x, w_kv, out_0, out_1, out_2):
             for i in range(passes):
                 nc.tensor.matmul(out=nowhere[:], lhsT=zeros[:, 0:P], rhs=zeros[:], start=True, stop=True)
 
+        sorted_words = {}
+
+        def sort_words(r):
+            g, in_group = divmod(r, ROUNDS_PER_GROUP)
+            row = x_tiles[g][:, in_group * ROUND * D : (in_group + 1) * ROUND * D].bitcast(F32)
+            apart = sorted_pool.tile([P, ROUND, 2, P], F32)
+            nc.vector.tensor_copy(out=apart[:], in_=row.rearrange("p (j w u) -> p j u w", j=ROUND, u=2))
+            sorted_words[r] = apart
+
         def transpose_round(r):
             g, in_group = divmod(r, ROUNDS_PER_GROUP)
             words = x_tiles[g][:].bitcast(F32)
@@ -94,9 +106,12 @@ def tile_ammattention_pa_t_kernel(tc, x, w_kv, out_0, out_1, out_2):
                 xt = xt_banks.tile([P, 2, 2, P], F32)
                 for jj in range(2):
                     for u in range(2):
-                        first = (in_group * ROUND + 2 * pair + jj) * WORDS
-                        every_second = slice(first + u, first + WORDS, 2)
-                        nc.tensor.transpose(xt[:, jj, u, :], words[:, every_second], ident[:])
+                        if r in sorted_words:
+                            word_run = sorted_words[r][:, 2 * pair + jj, u]
+                        else:
+                            first = (in_group * ROUND + 2 * pair + jj) * WORDS
+                            word_run = words[:, first + u : first + WORDS : 2]
+                        nc.tensor.transpose(xt[:, jj, u, :], word_run, ident[:])
                 nc.scalar.copy(
                     out=grouped_words[:, 2 * pair : 2 * pair + 2],
                     in_=xt[:].rearrange("p j u s -> p j s u"),
@@ -191,6 +206,8 @@ def tile_ammattention_pa_t_kernel(tc, x, w_kv, out_0, out_1, out_2):
                     keys_pass(r, jj)
                 elif r > 0:
                     multiply(tail_sum[:], r, jj, VALUES, jj == 0, jj == ROUND - 1)
+                if jj == ROUND // 2 and in_group == 1 and r + SORT_AHEAD < ROUNDS:
+                    sort_words(r + SORT_AHEAD)
                 v_bank = v_banks.tile([P, D], F32)
                 multiply(v_bank[:], r, jj, VALUES, True, True)
                 nc.scalar.copy(out=v_rows[:, jj * D : (jj + 1) * D], in_=v_bank[:])
@@ -198,7 +215,7 @@ def tile_ammattention_pa_t_kernel(tc, x, w_kv, out_0, out_1, out_2):
                     nc.sync.dma_start(out=v_groups[g, :, j * D : (j + 1) * D], in_=v_rows[:, jj * D : (jj + 1) * D])
                 elif jj % 2 == 1:
                     pair = v_rows[:, (jj - 1) * D : (jj + 1) * D]
-                    if g == GROUPS - 1:
+                    if r >= FINE:
                         nc.sync.dma_start(out=v_groups[g, :, (j - 1) * D : (j + 1) * D], in_=pair)
                     elif jj == ROUND - 1:
                         nc.sync.dma_start(out=v_groups[g, :, (j + 1 - ROUND) * D : (j + 1) * D], in_=v_rows[:])

from contextlib import ExitStack

import concourse.mybir as mybir
from concourse.masks import make_identity

F32 = mybir.dt.float32
BF16 = mybir.dt.bfloat16
U32 = mybir.dt.uint32
U8 = mybir.dt.uint8
FP8X4 = mybir.dt.float8_e4m3fn_x4

P = 128
PACK = 4
D = 512
WORDS = D // 2
TOKENS = 2 * 4096
SEG = 16
GROUPS = TOKENS // (P * SEG)
ROUND = 4
ROUNDS_PER_GROUP = SEG // ROUND
ROUNDS = GROUPS * ROUNDS_PER_GROUP
LOOKAHEAD = 2
KEYS = 0
VALUES = 1
SORT_AHEAD = 5
FINE = ROUNDS // 2
ADD = mybir.AluOpType.add
MULT = mybir.AluOpType.mult
SUM_NAMES = ("even_sum", "odd_sum")
COPY = mybir.ActivationFunctionType.Copy

FLOPS = 2 * TOKENS * D * 2 * D


def tile_ammattention_pa_t_kernel(tc, x, w_kv, out_0, out_1, out_2):
    nc = tc.nc

    x_groups = x.flatten_outer_dims().rearrange("(g s j) k -> g s (j k)", s=P, j=SEG)
    v_groups = out_0.flatten_outer_dims().rearrange("(g s j) d -> g s (j d)", s=P, j=SEG)
    keys_mean_groups = out_1.flatten_outer_dims().rearrange("(g s) d -> g s d", s=P)
    vals_mean_groups = out_2.flatten_outer_dims().rearrange("(g s) d -> g s d", s=P)

    with ExitStack() as ctx:
        const = ctx.enter_context(tc.tile_pool(name="const", bufs=1))
        x_pool = ctx.enter_context(tc.tile_pool(name="x", bufs=GROUPS))
        w_pool = ctx.enter_context(tc.tile_pool(name="w", bufs=2))
        grouped_pool = ctx.enter_context(tc.tile_pool(name="grouped", bufs=3))
        sorted_pool = ctx.enter_context(tc.tile_pool(name="sorted", bufs=2))
        mx_pool = ctx.enter_context(tc.tile_pool(name="mx", bufs=LOOKAHEAD + 2))
        v_pool = ctx.enter_context(tc.tile_pool(name="v", bufs=9))
        sum_pool = ctx.enter_context(tc.tile_pool(name="sum", bufs=2))
        xt_banks = ctx.enter_context(tc.psum_pool(name="xt", bufs=2))
        v_banks = ctx.enter_context(tc.psum_pool(name="vb", bufs=4))
        keys_banks = ctx.enter_context(tc.psum_pool(name="kb", bufs=2))
        ctx.enter_context(tc.manual_schedule())

        x_tiles = [x_pool.tile([P, SEG * D], BF16, name="x_tile") for g in range(GROUPS)]

        def load_x(g, first_round, rounds):
            cols = slice(first_round * ROUND * D, (first_round + rounds) * ROUND * D)
            nc.sync.dma_start(out=x_tiles[g][:, cols], in_=x_groups[g, :, cols])

        w_rows = [w_pool.tile([P, PACK, D], BF16, name="w_rows") for half in (KEYS, VALUES)]

        def load_w(half):
            cols = slice(half * D, (half + 1) * D)
            nc.sync.dma_start(
                out=w_rows[half][:], in_=w_kv.rearrange("(p t) c -> p t c", t=PACK)[:, :, cols]
            )

        load_x(0, 0, 1)
        load_w(VALUES)
        load_x(0, 1, 1)
        load_w(KEYS)
        for r in range(2, ROUNDS_PER_GROUP):
            load_x(0, r, 1)
        for g in range(1, GROUPS):
            load_x(g, 0, ROUNDS_PER_GROUP)

        ident = const.tile([P, P], F32)
        make_identity(nc, ident[:])

        zeros = const.tile([P, D], BF16)
        nc.vector.memset(zeros[:], 0.0)

        def warm_up(passes):
            nowhere = v_banks.tile([P, D], F32, name="v_bank")
            for i in range(passes):
                nc.tensor.matmul(out=nowhere[:], lhsT=zeros[:, 0:P], rhs=zeros[:], start=True, stop=True)

        sorted_words = {}

        def sort_words(r):
            g, in_group = divmod(r, ROUNDS_PER_GROUP)
            row = x_tiles[g][:, in_group * ROUND * D : (in_group + 1) * ROUND * D].bitcast(F32)
            apart = sorted_pool.tile([P, ROUND, 2, P], F32)
            nc.vector.tensor_copy(out=apart[:], in_=row.rearrange("p (j w u) -> p j u w", j=ROUND, u=2))
            sorted_words[r] = apart

        def transpose_round(r):
            g, in_group = divmod(r, ROUNDS_PER_GROUP)
            words = x_tiles[g][:].bitcast(F32)
            grouped = grouped_pool.tile([P, ROUND * P * PACK], BF16, align_bytes=64)
            grouped_words = grouped[:].bitcast(F32).rearrange("p (j s u) -> p j s u", j=ROUND, u=2)
            for pair in range(ROUND // 2):
                xt = xt_banks.tile([P, 2, 2, P], F32)
                for jj in range(2):
                    for u in range(2):
                        if r in sorted_words:
                            word_run = sorted_words[r][:, 2 * pair + jj, u]
                        else:
                            first = (in_group * ROUND + 2 * pair + jj) * WORDS
                            word_run = words[:, first + u : first + WORDS : 2]
                        nc.tensor.transpose(xt[:, jj, u, :], word_run, ident[:])
                nc.scalar.copy(
                    out=grouped_words[:, 2 * pair : 2 * pair + 2],
                    in_=xt[:].rearrange("p j u s -> p j s u"),
                )
            return grouped

        quantised = []

        def quantise_round(grouped):
            codes = mx_pool.tile([P, ROUND * P], U32, align_bytes=256)
            scales = mx_pool.tile([P, ROUND * P], U8, align_bytes=256)
            nc.vector.quantize_mx(out=codes[:].bitcast(FP8X4), scales=scales[:], in_=grouped[:])
            quantised.append((codes, scales))

        w_grouped = const.tile([P, 2, D, PACK], BF16, align_bytes=64)
        w_codes = const.tile([P, 2, D], U32, align_bytes=256)
        w_scales = const.tile([P, 2, D], U8, align_bytes=256)

        def regroup_w(half):
            nc.vector.tensor_copy(
                out=w_grouped[:, half].rearrange("p (c i) t -> p c t i", i=4),
                in_=w_rows[half][:].rearrange("p t (c i) -> p c t i", i=4),
            )

        def quantise_w(half):
            nc.vector.quantize_mx(
                out=w_codes[:, half].bitcast(FP8X4),
                scales=w_scales[:, half],
                in_=w_grouped[:, half].rearrange("p c t -> p (c t)"),
            )

        warm_up(5)
        grouped = transpose_round(0)
        regroup_w(VALUES)
        quantise_round(grouped)
        quantise_w(VALUES)
        warm_up(3)
        grouped = transpose_round(1)
        warm_up(2)
        regroup_w(KEYS)
        quantise_w(KEYS)
        quantise_round(grouped)

        def multiply(out, r, jj, half, start, stop):
            codes, scales = quantised[r]
            segs = slice(jj * P, (jj + 1) * P)
            nc.tensor.matmul_mx(
                out=out,
                lhsT=codes[:, segs].bitcast(FP8X4),
                lhsT_scale=scales[:, segs],
                rhs=w_codes[:, half].bitcast(FP8X4),
                rhs_scale=w_scales[:, half],
                start=start,
                stop=stop,
            )

        keys_sums = {}

        def keys_pass(r, jj):
            g, j = divmod(r * ROUND + jj, SEG)
            if j == 0:
                keys_sums[g] = keys_banks.tile([P, D], F32, name="keys_sum")
            multiply(keys_sums[g][:], r, jj, KEYS, j == 0, j == SEG - 1)
            if j == SEG - 1:
                keys_mean = sum_pool.tile([P, D], F32)
                if g < GROUPS - 1:
                    nc.vector.tensor_scalar_mul(out=keys_mean[:], in0=keys_sums[g][:], scalar1=1.0 / SEG)
                    nc.gpsimd.dma_start(out=keys_mean_groups[g], in_=keys_mean[:])
                else:
                    nc.scalar.activation(out=keys_mean[:], in_=keys_sums[g][:], func=COPY, scale=1.0 / SEG)
                    nc.sync.dma_start(out=keys_mean_groups[g], in_=keys_mean[:])

        first_pair = None
        vals_sum = None
        last_sums = [None, None]
        tail_sum = None
        for r in range(ROUNDS):
            g, in_group = divmod(r, ROUNDS_PER_GROUP)
            if 0 < r < ROUNDS - LOOKAHEAD:
                quantise_round(transpose_round(r + LOOKAHEAD))

            if in_group == 0 and g < GROUPS - 1:
                vals_sum = sum_pool.tile([P, 2 * D], F32)
            if r == ROUNDS - 1:
                for jj in range(ROUND):
                    keys_pass(r, jj)
                tail_sum = xt_banks.tile([P, D], F32, name="xt")
            v_rows = v_pool.tile([P, ROUND * D], F32)
            for jj in range(ROUND):
                j = in_group * ROUND + jj
                if 0 < r < ROUNDS - 1:
                    keys_pass(r, jj)
                elif r > 0:
                    multiply(tail_sum[:], r, jj, VALUES, jj == 0, jj == ROUND - 1)
                if jj == ROUND // 2 and in_group == 1 and r + SORT_AHEAD < ROUNDS:
                    sort_words(r + SORT_AHEAD)
                v_bank = v_banks.tile([P, D], F32)
                multiply(v_bank[:], r, jj, VALUES, True, True)
                nc.scalar.copy(out=v_rows[:, jj * D : (jj + 1) * D], in_=v_bank[:])
                if r == ROUNDS - 1 and jj >= ROUND - 2:
                    nc.sync.dma_start(out=v_groups[g, :, j * D : (j + 1) * D], in_=v_rows[:, jj * D : (jj + 1) * D])
                elif jj % 2 == 1:
                    pair = v_rows[:, (jj - 1) * D : (jj + 1) * D]
                    if r >= FINE:
                        nc.sync.dma_start(out=v_groups[g, :, (j - 1) * D : (j + 1) * D], in_=pair)
                    elif jj == ROUND - 1:
                        nc.sync.dma_start(out=v_groups[g, :, (j + 1 - ROUND) * D : (j + 1) * D], in_=v_rows[:])
                    if j == 1:
                        first_pair = pair
                    elif g < GROUPS - 1:
                        before = first_pair if j == 3 else vals_sum[:]
                        nc.vector.tensor_add(out=vals_sum[:], in0=before, in1=pair)
                if g == GROUPS - 1 and r < ROUNDS - 1:
                    before = last_sums[jj % 2]
                    v_slice = v_rows[:, jj * D : (jj + 1) * D]
                    if j < 2:
                        last_sums[jj % 2] = v_slice
                    else:
                        if j < 4:
                            running = sum_pool.tile([P, D], F32, name=SUM_NAMES[jj % 2])
                            last_sums[jj % 2] = running[:]
                        nc.vector.tensor_add(out=last_sums[jj % 2], in0=before, in1=v_slice)
            if r == 0:
                quantise_round(transpose_round(LOOKAHEAD))
                for jj in range(ROUND):
                    keys_pass(r, jj)
            if in_group == ROUNDS_PER_GROUP - 1 and g < GROUPS - 1:
                mean = sum_pool.tile([P, D], F32, name="vals_mean")
                nc.vector.tensor_add(out=mean[:], in0=vals_sum[:, 0:D], in1=vals_sum[:, D : 2 * D])
                nc.vector.tensor_scalar_mul(out=mean[:], in0=mean[:], scalar1=1.0 / SEG)
                nc.gpsimd.dma_start(out=vals_mean_groups[g], in_=mean[:])
        mean = sum_pool.tile([P, D], F32, name="vals_mean")
        nc.vector.tensor_add(out=mean[:], in0=last_sums[0], in1=last_sums[1])
        nc.vector.tensor_scalar_mul(out=mean[:], in0=mean[:], scalar1=1.0 / SEG)
        nc.vector.scalar_tensor_tensor(
            out=mean[:], in0=tail_sum[:], scalar=1.0 / SEG, op0=MULT, in1=mean[:], op1=ADD
        )
        nc.sync.dma_start(out=vals_mean_groups[GROUPS - 1], in_=mean[:])
